import numpy as np
import ml_dtypes


def mxq(x, axis, fmt="e4m3"):
    dtype, down = {"e4m3": (ml_dtypes.float8_e4m3fn, 7), "e5m2": (ml_dtypes.float8_e5m2, 14)}[fmt]
    v = np.moveaxis(np.asarray(x, np.float32).astype(ml_dtypes.bfloat16).astype(np.float64), axis, -1)
    blocks = v.reshape(v.shape[:-1] + (-1, 32))
    amax = np.abs(blocks).max(-1, keepdims=True)
    byte = np.maximum(np.where(amax > 0, np.frexp(amax)[1] - 1 + 127, 0) - down, 1)
    scale = np.exp2(byte - 127.0)
    codes = (blocks / scale).astype(np.float32).astype(dtype).astype(np.float64)
    return np.moveaxis((codes * scale).reshape(v.shape), -1, axis)


WIDE = False


def mx_kscale(k):
    if not WIDE:
        return np.ones(k)
    levels = np.array([10, -10, 5, -5, 0])
    a = np.random.permutation(np.resize(levels, k // 512 * 4)).reshape(k // 512, 4)
    idx = np.arange(k)
    return np.exp2(a[idx // 512, idx % 128 // 32])


BF16 = ml_dtypes.bfloat16


def bf(x):
    return np.asarray(x, np.float32).astype(BF16)


def f64(x):
    return np.asarray(x).astype(np.float64)


B, T, D, H, DH, R, F = 2, 4096, 512, 2, 128, 32, 4096
EPS = 1e-5
E = H * DH


def rope(u, c, s):
    ur, up = u[..., :R], u[..., R:]
    c = c[None, :, None, :]
    s = s[None, :, None, :]
    ue, uo = ur[..., ::2], ur[..., 1::2]
    ur2 = np.stack([ue * c - uo * s, uo * c + ue * s], axis=-1).reshape(ur.shape)
    return np.concatenate([ur2, up], axis=-1)


def setup_inputs():
    rn = np.random.standard_normal
    s = mx_kscale(D)
    ang = np.random.uniform(0.0, 2.0 * np.pi, (T, R // 2))
    return {
        "x": bf(3.0 * np.sqrt(EPS) * (rn((B, T, D)) + 0.5 * rn((B, T, 1)))),
        "ln_scale": bf((1.0 + 0.1 * rn(D)) * s),
        "ln_offset": bf(0.1 * rn(D) * s),
        "wq": bf(rn((D, E)) / np.sqrt(D) / s[:, None]),
        "wk": bf(rn((D, E)) / np.sqrt(D) / s[:, None]),
        "wv": bf(rn((D, E)) / np.sqrt(D) / s[:, None]),
        "rope_cos": bf(np.cos(ang)),
        "rope_sin": bf(np.sin(ang)),
    }


def reference(x, ln_scale, ln_offset, wq, wk, wv, rope_cos, rope_sin):
    x = f64(x)
    mean = x.mean(-1, keepdims=True)
    var = ((x - mean) ** 2).mean(-1, keepdims=True)
    xn = (x - mean) * (1.0 / np.sqrt(var + EPS))
    xn = xn * f64(ln_scale) + f64(ln_offset)
    xq = mxq(xn, 2, "e4m3")
    q = (xq @ mxq(f64(wq), 0, "e4m3")).reshape(B, T, H, DH)
    k = (xq @ mxq(f64(wk), 0, "e4m3")).reshape(B, T, H, DH)
    v = (xq @ mxq(f64(wv), 0, "e4m3")).reshape(B, T, H, DH)
    c, s = f64(rope_cos), f64(rope_sin)
    return rope(q, c, s), rope(k, c, s), v

@@ -1,0 +1,311 @@
+from contextlib import ExitStack
+
+import concourse.mybir as mybir
+from concourse.masks import make_identity
+
+F32 = mybir.dt.float32
+BF16 = mybir.dt.bfloat16
+U32 = mybir.dt.uint32
+U8 = mybir.dt.uint8
+FP8X4 = mybir.dt.float8_e4m3fn_x4
+ALU = mybir.AluOpType
+ACT = mybir.ActivationFunctionType
+
+P = 128
+PACK = 4
+B, T, D, H, DH, ROT = 2, 4096, 512, 2, 128, 32
+E = H * DH
+EPS = 1e-5
+TOKENS = B * T
+TILES = 4
+MACRO = P * TILES
+N_MACRO = TOKENS // MACRO
+POS_MACRO = T // MACRO
+HALF = ROT // 2
+HEADS_QK = 2 * H
+
+ROPE_COLS = 2 * HEADS_QK * ROT
+V_COLS = E
+PASS_COLS = HEADS_QK * (DH - ROT)
+ROPE_AT = 0
+V_AT = ROPE_AT + ROPE_COLS
+PASS_AT = V_AT + V_COLS
+W_COLS = PASS_AT + PASS_COLS
+
+FLOPS = 2 * TOKENS * D * 3 * E
+
+
+LOAD_AHEAD = 6
+STATS_AHEAD = 5
+RSTD_AHEAD = 4
+Z_AHEAD = 3
+PLANES_AHEAD = 2
+QUANT_AHEAD = 1
+
+
+def tile_transformerlayershard_pa_t_kernel(
+    tc, x, ln_scale, ln_offset, wq, wk, wv, rope_cos, rope_sin, out_0, out_1, out_2
+):
+    nc = tc.nc
+    x_rows = x.rearrange("b t k -> (b t) k").rearrange("(m p i) k -> m p (i k)", p=P, i=TILES)
+    out_rows = [
+        o.rearrange("b t h d -> (b t) (h d)").rearrange("(m p i) c -> m p (i c)", p=P, i=TILES)
+        for o in (out_0, out_1, out_2)
+    ]
+
+    with ExitStack() as ctx:
+        const = ctx.enter_context(tc.tile_pool(name="const", bufs=1))
+        x_pool = ctx.enter_context(tc.tile_pool(name="x", bufs=5))
+        small = ctx.enter_context(tc.tile_pool(name="small", bufs=4))
+        z_pool = ctx.enter_context(tc.tile_pool(name="z", bufs=3))
+        work = ctx.enter_context(tc.tile_pool(name="work", bufs=2))
+        stage_pool = ctx.enter_context(tc.tile_pool(name="stage", bufs=3))
+        psum_t = ctx.enter_context(tc.psum_pool(name="psum_t", bufs=4))
+        psum_o = ctx.enter_context(tc.psum_pool(name="psum_o", bufs=4))
+        ctx.enter_context(tc.manual_schedule())
+
+        x_of, stats_of, mean_var_of, var_eps_of, std_of, rstd_of, neg_mean_of = {}, {}, {}, {}, {}, {}, {}
+        z_of, planes_ps_of, planes_of, grouped_of, codes_of, scales_of = {}, {}, {}, {}, {}, {}
+        banks_of, stage_of, products_of = {}, {}, {}
+
+        def load(m):
+            x_of[m] = x_pool.tile([P, TILES, D], BF16, name="x_sb")
+            nc.sync.dma_start(out=x_of[m][:].rearrange("p i k -> p (i k)"), in_=x_rows[m])
+
+        load(0)
+
+        ident = const.tile([P, P], F32)
+        make_identity(nc, ident[:])
+
+        w_raw = []
+        for o, w in enumerate((wq, wk, wv)):
+            w_sb = const.tile([P, PACK, E], BF16, name="w_raw%d" % o)
+            nc.sync.dma_start(out=w_sb[:], in_=w.rearrange("(j p) n -> p j n", p=P))
+            w_raw.append(w_sb)
+
+        affine_rows = const.tile([P, P], BF16)
+        nc.vector.memset(affine_rows[:], 0.0)
+        nc.scalar.dma_start(out=affine_rows[0:PACK, :], in_=ln_scale.rearrange("(j p) -> j p", p=P))
+        nc.scalar.dma_start(out=affine_rows[PACK : 2 * PACK, :], in_=ln_offset.rearrange("(j p) -> j p", p=P))
+        affine_rows_f32 = const.tile([P, P], F32)
+        nc.vector.tensor_copy(out=affine_rows_f32[:], in_=affine_rows[:])
+        affine_ps = psum_t.tile([P, MACRO], F32, tag="plane")
+        nc.tensor.transpose(affine_ps[:, 0:P], affine_rows_f32[:], ident[:])
+        affine = const.tile([P, 2 * PACK], F32)
+        nc.vector.tensor_copy(out=affine[:], in_=affine_ps[:, 0 : 2 * PACK])
+
+        rot = const.tile([P, POS_MACRO * TILES, 2, ROT], F32)
+        for c, table in enumerate((rope_cos, rope_sin)):
+            raw = const.tile([P, POS_MACRO, TILES * HALF], BF16, name="rot_raw%d" % c)
+            nc.scalar.dma_start(out=raw[:], in_=table.rearrange("(m p i) a -> p m (i a)", p=P, i=TILES))
+            nc.scalar.copy(
+                out=rot[:, :, c, :].rearrange("p t (a e) -> p t a e", e=2),
+                in_=raw[:]
+                .rearrange("p m (i a) -> p (m i) a", a=HALF)
+                .unsqueeze(3)
+                .to_broadcast([P, POS_MACRO * TILES, HALF, 2]),
+            )
+
+        w_grouped = const.tile([P, W_COLS, PACK], BF16, align_bytes=64)
+        w_codes = const.tile([P, W_COLS], U32, align_bytes=64)
+        w_scales = const.tile([P, W_COLS], U8, align_bytes=64)
+
+        def regroup_weights():
+            for o in range(2):
+                by_col = w_raw[o][:].rearrange("p j (h d) -> p h d j", h=H)
+                head_cols = H * ROT
+                plain_at = ROPE_AT + o * head_cols
+                nc.scalar.copy(
+                    out=w_grouped[:, plain_at : plain_at + head_cols, :].rearrange("p (h f) j -> p h f j", h=H),
+                    in_=by_col[:, :, 0:ROT, :],
+                )
+                swap_at = ROPE_AT + HEADS_QK * ROT + o * head_cols
+                swapped = w_grouped[:, swap_at : swap_at + head_cols, :].rearrange(
+                    "p (h a e) j -> p h a e j", h=H, e=2
+                )
+                pairs = by_col[:, :, 0:ROT, :].rearrange("p h (a e) j -> p h a e j", e=2)
+                nc.scalar.mul(out=swapped[:, :, :, 0, :], in_=pairs[:, :, :, 1, :], mul=-1.0)
+                nc.scalar.copy(out=swapped[:, :, :, 1, :], in_=pairs[:, :, :, 0, :])
+                pass_cols = H * (DH - ROT)
+                pass_at = PASS_AT + o * pass_cols
+                nc.scalar.copy(
+                    out=w_grouped[:, pass_at : pass_at + pass_cols, :].rearrange("p (h d) j -> p h d j", h=H),
+                    in_=by_col[:, :, ROT:DH, :],
+                )
+            nc.scalar.copy(out=w_grouped[:, V_AT : V_AT + V_COLS, :], in_=w_raw[2][:].rearrange("p j n -> p n j"))
+
+        def quantise_weights():
+            for lo, hi in ((0, 512), (512, 768), (768, 896)):
+                nc.vector.quantize_mx(
+                    out=w_codes[:, lo:hi].bitcast(FP8X4),
+                    scales=w_scales[:, lo:hi],
+                    in_=w_grouped[:, lo:hi, :].rearrange("p c j -> p (c j)"),
+                )
+
+        def token_stats(m, half):
+            if half == 0:
+                stats_of[m] = small.tile([P, TILES, 6], F32, name="stats")
+                mean_var_of[m] = small.tile([P, TILES, 2], F32, name="mean_var")
+            for i in (2 * half, 2 * half + 1):
+                nc.vector.bn_stats(out=stats_of[m][:, i, :], in_=x_of[m][:, i, :])
+            for i in (2 * half, 2 * half + 1):
+                nc.vector.bn_aggr(out=mean_var_of[m][:, i, :], in_=stats_of[m][:, i, :])
+            if half == 1:
+                var_eps_of[m] = small.tile([P, TILES], F32, name="var_eps")
+                nc.vector.tensor_scalar(
+                    out=var_eps_of[m][:], in0=mean_var_of[m][:, :, 1], scalar1=EPS, scalar2=None, op0=ALU.add
+                )
+
+        def std_dev(m):
+            std_of[m] = small.tile([P, TILES], F32, name="std")
+            nc.scalar.activation(out=std_of[m][:], in_=var_eps_of[m][:], func=ACT.Sqrt)
+
+        def inverse_std(m):
+            rstd_of[m] = small.tile([P, TILES], F32, name="rstd")
+            nc.vector.reciprocal(out=rstd_of[m][:], in_=std_of[m][:])
+            neg_mean_of[m] = small.tile([P, TILES], F32, name="neg_mean")
+            nc.vector.tensor_scalar(
+                out=neg_mean_of[m][:], in0=mean_var_of[m][:, :, 0], scalar1=-1.0, scalar2=None, op0=ALU.mult
+            )
+
+        def normalise(m):
+            z_of[m] = z_pool.tile([P, TILES, D], F32, name="z")
+            for i in range(TILES):
+                nc.gpsimd.tensor_scalar(
+                    out=z_of[m][:, i, :],
+                    in0=x_of[m][:, i, :],
+                    scalar1=neg_mean_of[m][:, i : i + 1],
+                    scalar2=rstd_of[m][:, i : i + 1],
+                    op0=ALU.add,
+                    op1=ALU.mult,
+                )
+
+        def transpose(m):
+            planes_ps_of[m] = [
+                psum_t.tile([P, MACRO], F32, tag="plane", name="plane_ps%d" % j) for j in range(PACK)
+            ]
+            for j in range(PACK):
+                for i in range(TILES):
+                    nc.tensor.transpose(
+                        planes_ps_of[m][j][:, i * P : (i + 1) * P], z_of[m][:, i, j * P : (j + 1) * P], ident[:]
+                    )
+
+        def scale_shift(m):
+            planes_of[m] = work.tile([P, PACK, MACRO], BF16, name="xn_planes")
+            for j in range(PACK):
+                nc.scalar.activation(
+                    out=planes_of[m][:, j, :],
+                    in_=planes_ps_of[m][j][:],
+                    func=ACT.Identity,
+                    scale=affine[:, j : j + 1],
+                    bias=affine[:, PACK + j : PACK + j + 1],
+                )
+
+        def regroup(m):
+            grouped_of[m] = work.tile([P, MACRO, PACK], BF16, align_bytes=64, name="xn_grouped")
+            nc.vector.tensor_copy(
+                out=grouped_of[m][:].rearrange("p (c r) j -> p c j r", r=4),
+                in_=planes_of[m][:].rearrange("p j (c r) -> p c j r", r=4),
+            )
+
+        def quantise(m):
+            codes_of[m] = work.tile([P, MACRO], U32, align_bytes=64, name="xn_codes")
+            scales_of[m] = work.tile([P, MACRO], U8, align_bytes=64, name="xn_scales")
+            nc.vector.quantize_mx(
+                out=codes_of[m][:].bitcast(FP8X4),
+                scales=scales_of[m][:],
+                in_=grouped_of[m][:].rearrange("p t j -> p (t j)"),
+            )
+
+        def one_pass(m, i, out_ps, at, cols):
+            nc.tensor.matmul_mx(
+                out=out_ps,
+                lhsT=codes_of[m][:, i * P : (i + 1) * P].bitcast(FP8X4),
+                lhsT_scale=scales_of[m][:, i * P : (i + 1) * P],
+                rhs=w_codes[:, at : at + cols].bitcast(FP8X4),
+                rhs_scale=w_scales[:, at : at + cols],
+                start=True,
+                stop=True,
+            )
+
+        def project(m, pair):
+            first = 2 * pair
+            v_ps = psum_o.tile([P, 512], F32, tag="out")
+            pass_ps = [psum_o.tile([P, 512], F32, tag="out", name="pass_ps%d" % n) for n in range(2)]
+            rope_ps = psum_o.tile([P, 512], F32, tag="out")
+            banks_of[(m, pair)] = (v_ps, pass_ps, rope_ps)
+            for n in range(2):
+                one_pass(m, first + n, v_ps[:, n * V_COLS : (n + 1) * V_COLS], V_AT, V_COLS)
+            for n in range(2):
+                one_pass(m, first + n, pass_ps[n][:, 0:256], PASS_AT, 256)
+                one_pass(m, first + n, pass_ps[n][:, 256:PASS_COLS], PASS_AT + 256, PASS_COLS - 256)
+            for n in range(2):
+                one_pass(m, first + n, rope_ps[:, n * ROPE_COLS : (n + 1) * ROPE_COLS], ROPE_AT, ROPE_COLS)
+
+        def copy_out(m, pair):
+            first = 2 * pair
+            if pair == 0:
+                stage_of[m] = stage_pool.tile([P, 3, TILES, E], F32, name="stage")
+            stage = stage_of[m]
+            v_ps, pass_ps, rope_ps = banks_of[(m, pair)]
+            nc.scalar.copy(out=stage[:, 2, first : first + 2, :].rearrange("p i c -> p (i c)"), in_=v_ps[:])
+            for n in range(2):
+                nc.scalar.copy(
+                    out=stage[:, 0:2, first + n, :].rearrange("p o (h d) -> p o h d", h=H)[:, :, :, ROT:DH],
+                    in_=pass_ps[n][:, 0:PASS_COLS].rearrange("p (o h d) -> p o h d", o=2, h=H),
+                )
+
+        def rope_products(m, pair):
+            first = 2 * pair
+            if pair == 0:
+                products_of[m] = work.tile([P, TILES, 2, HEADS_QK, ROT], F32, name="products")
+            v_ps, pass_ps, rope_ps = banks_of[(m, pair)]
+            pos = (m % POS_MACRO) * TILES + first
+            nc.vector.tensor_tensor(
+                out=products_of[m][:, first : first + 2, :, :, :].rearrange("p i c g f -> p (i c) g f"),
+                in0=rope_ps[:].rearrange("p (a g f) -> p a g f", g=HEADS_QK, f=ROT),
+                in1=rot[:, pos : pos + 2, :, :]
+                .rearrange("p i c f -> p (i c) f")
+                .unsqueeze(2)
+                .to_broadcast([P, 4, HEADS_QK, ROT]),
+                op=ALU.mult,
+            )
+
+        def rotate_and_store(m):
+            for o in range(2):
+                nc.gpsimd.tensor_tensor(
+                    out=stage_of[m][:, o, :, :].rearrange("p i (h d) -> p i h d", h=H)[:, :, :, 0:ROT],
+                    in0=products_of[m][:, :, 0, o * H : (o + 1) * H, :],
+                    in1=products_of[m][:, :, 1, o * H : (o + 1) * H, :],
+                    op=ALU.add,
+                )
+            for o in range(3):
+                nc.sync.dma_start(out=out_rows[o][m], in_=stage_of[m][:, o, :, :].rearrange("p i c -> p (i c)"))
+
+        def when(m, stage, *args):
+            if 0 <= m < N_MACRO:
+                stage(m, *args)
+
+        for s in range(-LOAD_AHEAD, N_MACRO + 1):
+            if s + LOAD_AHEAD > 0:
+                when(s + LOAD_AHEAD, load)
+            when(s, project, 0)
+            when(s, copy_out, 0)
+            when(s + RSTD_AHEAD, std_dev)
+            if s + RSTD_AHEAD == 0:
+                regroup_weights()
+            when(s + PLANES_AHEAD, transpose)
+            when(s - 1, rotate_and_store)
+            when(s + Z_AHEAD, normalise)
+            when(s + QUANT_AHEAD, regroup)
+            when(s, rope_products, 0)
+            when(s + RSTD_AHEAD, inverse_std)
+            when(s + PLANES_AHEAD, scale_shift)
+            when(s, project, 1)
+            when(s + STATS_AHEAD, token_stats, 0)
+            when(s + QUANT_AHEAD, quantise)
+            when(s, rope_products, 1)
+            when(s, copy_out, 1)
+            when(s + STATS_AHEAD, token_stats, 1)
+            if s + PLANES_AHEAD == 0:
+                quantise_weights()

@@ -13,6 +13,8 @@ ACT = mybir.ActivationFunctionType
 
 P = 128
 PACK = 4
+BANK = 512
+BANKS = 8
 B, T, D, H, DH, ROT = 2, 4096, 512, 2, 128, 32
 E = H * DH
 EPS = 1e-5
@@ -34,13 +36,13 @@ W_COLS = PASS_AT + PASS_COLS
 
 FLOPS = 2 * TOKENS * D * 3 * E
 
-
 LOAD_AHEAD = 6
-STATS_AHEAD = 5
-RSTD_AHEAD = 4
-Z_AHEAD = 3
+STATS_AHEAD = 4
+NORM_AHEAD = 3
 PLANES_AHEAD = 2
 QUANT_AHEAD = 1
+
+GPSIMD_TILES = 3
 
 
 def tile_transformerlayershard_pa_t_kernel(
@@ -59,12 +61,14 @@ def tile_transformerlayershard_pa_t_kernel(
         small = ctx.enter_context(tc.tile_pool(name="small", bufs=4))
         z_pool = ctx.enter_context(tc.tile_pool(name="z", bufs=3))
         work = ctx.enter_context(tc.tile_pool(name="work", bufs=2))
-        stage_pool = ctx.enter_context(tc.tile_pool(name="stage", bufs=3))
-        psum_t = ctx.enter_context(tc.psum_pool(name="psum_t", bufs=4))
-        psum_o = ctx.enter_context(tc.psum_pool(name="psum_o", bufs=4))
+        out_pool = ctx.enter_context(tc.tile_pool(name="out", bufs=3))
+        psum = ctx.enter_context(tc.psum_pool(name="psum", bufs=BANKS))
         ctx.enter_context(tc.manual_schedule())
 
-        x_of, stats_of, mean_var_of, var_eps_of, std_of, rstd_of, neg_mean_of = {}, {}, {}, {}, {}, {}, {}
+        def bank(name):
+            return psum.tile([P, BANK], F32, tag="bank", name=name)
+
+        x_of, stats_of, mean_var_of, var_eps_of, std_of, rstd_of, neg_mean_of, shift_of = {}, {}, {}, {}, {}, {}, {}, {}
         z_of, planes_ps_of, planes_of, grouped_of, codes_of, scales_of = {}, {}, {}, {}, {}, {}
         banks_of, stage_of, products_of = {}, {}, {}
 
@@ -73,6 +77,11 @@ def tile_transformerlayershard_pa_t_kernel(
             nc.sync.dma_start(out=x_of[m][:].rearrange("p i k -> p (i k)"), in_=x_rows[m])
 
         load(0)
+
+        one_col = const.tile([P, 1], F32)
+        nc.vector.memset(one_col[:], 1.0)
+        first_sqrt = const.tile([P, 1], F32)
+        nc.scalar.activation(out=first_sqrt[:], in_=one_col[:], func=ACT.Sqrt)
 
         ident = const.tile([P, P], F32)
         make_identity(nc, ident[:])
@@ -88,11 +97,11 @@ def tile_transformerlayershard_pa_t_kernel(
         nc.scalar.dma_start(out=affine_rows[0:PACK, :], in_=ln_scale.rearrange("(j p) -> j p", p=P))
         nc.scalar.dma_start(out=affine_rows[PACK : 2 * PACK, :], in_=ln_offset.rearrange("(j p) -> j p", p=P))
         affine_rows_f32 = const.tile([P, P], F32)
-        nc.vector.tensor_copy(out=affine_rows_f32[:], in_=affine_rows[:])
-        affine_ps = psum_t.tile([P, MACRO], F32, tag="plane")
+        nc.scalar.copy(out=affine_rows_f32[:], in_=affine_rows[:])
+        affine_ps = bank("affine_ps")
         nc.tensor.transpose(affine_ps[:, 0:P], affine_rows_f32[:], ident[:])
         affine = const.tile([P, 2 * PACK], F32)
-        nc.vector.tensor_copy(out=affine[:], in_=affine_ps[:, 0 : 2 * PACK])
+        nc.scalar.copy(out=affine[:], in_=affine_ps[:, 0 : 2 * PACK])
 
         rot = const.tile([P, POS_MACRO * TILES, 2, ROT], F32)
         for c, table in enumerate((rope_cos, rope_sin)):
@@ -110,29 +119,28 @@ def tile_transformerlayershard_pa_t_kernel(
         w_codes = const.tile([P, W_COLS], U32, align_bytes=64)
         w_scales = const.tile([P, W_COLS], U8, align_bytes=64)
 
-        def regroup_weights():
-            for o in range(2):
-                by_col = w_raw[o][:].rearrange("p j (h d) -> p h d j", h=H)
-                head_cols = H * ROT
-                plain_at = ROPE_AT + o * head_cols
-                nc.scalar.copy(
-                    out=w_grouped[:, plain_at : plain_at + head_cols, :].rearrange("p (h f) j -> p h f j", h=H),
-                    in_=by_col[:, :, 0:ROT, :],
-                )
-                swap_at = ROPE_AT + HEADS_QK * ROT + o * head_cols
-                swapped = w_grouped[:, swap_at : swap_at + head_cols, :].rearrange(
-                    "p (h a e) j -> p h a e j", h=H, e=2
-                )
-                pairs = by_col[:, :, 0:ROT, :].rearrange("p h (a e) j -> p h a e j", e=2)
-                nc.scalar.mul(out=swapped[:, :, :, 0, :], in_=pairs[:, :, :, 1, :], mul=-1.0)
-                nc.scalar.copy(out=swapped[:, :, :, 1, :], in_=pairs[:, :, :, 0, :])
-                pass_cols = H * (DH - ROT)
-                pass_at = PASS_AT + o * pass_cols
-                nc.scalar.copy(
-                    out=w_grouped[:, pass_at : pass_at + pass_cols, :].rearrange("p (h d) j -> p h d j", h=H),
-                    in_=by_col[:, :, ROT:DH, :],
-                )
-            nc.scalar.copy(out=w_grouped[:, V_AT : V_AT + V_COLS, :], in_=w_raw[2][:].rearrange("p j n -> p n j"))
+        def regroup_weights(o):
+            if o == 2:
+                nc.scalar.copy(out=w_grouped[:, V_AT : V_AT + V_COLS, :], in_=w_raw[2][:].rearrange("p j n -> p n j"))
+                return
+            by_col = w_raw[o][:].rearrange("p j (h d) -> p h d j", h=H)
+            head_cols = H * ROT
+            plain_at = ROPE_AT + o * head_cols
+            nc.scalar.copy(
+                out=w_grouped[:, plain_at : plain_at + head_cols, :].rearrange("p (h f) j -> p h f j", h=H),
+                in_=by_col[:, :, 0:ROT, :],
+            )
+            swap_at = ROPE_AT + HEADS_QK * ROT + o * head_cols
+            swapped = w_grouped[:, swap_at : swap_at + head_cols, :].rearrange("p (h a e) j -> p h a e j", h=H, e=2)
+            pairs = by_col[:, :, 0:ROT, :].rearrange("p h (a e) j -> p h a e j", e=2)
+            nc.scalar.mul(out=swapped[:, :, :, 0, :], in_=pairs[:, :, :, 1, :], mul=-1.0)
+            nc.scalar.copy(out=swapped[:, :, :, 1, :], in_=pairs[:, :, :, 0, :])
+            pass_cols = H * (DH - ROT)
+            pass_at = PASS_AT + o * pass_cols
+            nc.scalar.copy(
+                out=w_grouped[:, pass_at : pass_at + pass_cols, :].rearrange("p (h d) j -> p h d j", h=H),
+                in_=by_col[:, :, ROT:DH, :],
+            )
 
         def quantise_weights():
             for lo, hi in ((0, 512), (512, 768), (768, 896)):
@@ -142,35 +150,44 @@ def tile_transformerlayershard_pa_t_kernel(
                     in_=w_grouped[:, lo:hi, :].rearrange("p c j -> p (c j)"),
                 )
 
-        def token_stats(m, half):
-            if half == 0:
+        def token_stats(m, i):
+            if i == 0:
                 stats_of[m] = small.tile([P, TILES, 6], F32, name="stats")
-                mean_var_of[m] = small.tile([P, TILES, 2], F32, name="mean_var")
-            for i in (2 * half, 2 * half + 1):
-                nc.vector.bn_stats(out=stats_of[m][:, i, :], in_=x_of[m][:, i, :])
-            for i in (2 * half, 2 * half + 1):
+            nc.vector.bn_stats(out=stats_of[m][:, i, :], in_=x_of[m][:, i, :])
+
+        def mean_and_variance(m):
+            mean_var_of[m] = small.tile([P, TILES, 2], F32, name="mean_var")
+            for i in range(TILES):
                 nc.vector.bn_aggr(out=mean_var_of[m][:, i, :], in_=stats_of[m][:, i, :])
-            if half == 1:
-                var_eps_of[m] = small.tile([P, TILES], F32, name="var_eps")
-                nc.vector.tensor_scalar(
-                    out=var_eps_of[m][:], in0=mean_var_of[m][:, :, 1], scalar1=EPS, scalar2=None, op0=ALU.add
-                )
+            var_eps_of[m] = small.tile([P, TILES], F32, name="var_eps")
+            nc.vector.tensor_scalar(
+                out=var_eps_of[m][:], in0=mean_var_of[m][:, :, 1], scalar1=EPS, scalar2=None, op0=ALU.add
+            )
 
         def std_dev(m):
             std_of[m] = small.tile([P, TILES], F32, name="std")
             nc.scalar.activation(out=std_of[m][:], in_=var_eps_of[m][:], func=ACT.Sqrt)
 
+        def negate_mean(m):
+            neg_mean_of[m] = small.tile([P, TILES], F32, name="neg_mean")
+            nc.gpsimd.tensor_scalar(
+                out=neg_mean_of[m][:], in0=mean_var_of[m][:, :, 0], scalar1=-1.0, scalar2=0.0, op0=ALU.mult, op1=ALU.add
+            )
+
         def inverse_std(m):
             rstd_of[m] = small.tile([P, TILES], F32, name="rstd")
             nc.vector.reciprocal(out=rstd_of[m][:], in_=std_of[m][:])
-            neg_mean_of[m] = small.tile([P, TILES], F32, name="neg_mean")
-            nc.vector.tensor_scalar(
-                out=neg_mean_of[m][:], in0=mean_var_of[m][:, :, 0], scalar1=-1.0, scalar2=None, op0=ALU.mult
-            )
 
-        def normalise(m):
+        def normalise_on_gpsimd(m):
             z_of[m] = z_pool.tile([P, TILES, D], F32, name="z")
-            for i in range(TILES):
+            shift_of[m] = small.tile([P, TILES - GPSIMD_TILES], F32, name="shift")
+            nc.gpsimd.tensor_tensor(
+                out=shift_of[m][:],
+                in0=neg_mean_of[m][:, GPSIMD_TILES:TILES],
+                in1=rstd_of[m][:, GPSIMD_TILES:TILES],
+                op=ALU.mult,
+            )
+            for i in range(GPSIMD_TILES):
                 nc.gpsimd.tensor_scalar(
                     out=z_of[m][:, i, :],
                     in0=x_of[m][:, i, :],
@@ -180,10 +197,18 @@ def tile_transformerlayershard_pa_t_kernel(
                     op1=ALU.mult,
                 )
 
+        def normalise_on_scalar(m):
+            for i in range(GPSIMD_TILES, TILES):
+                nc.scalar.activation(
+                    out=z_of[m][:, i, :],
+                    in_=x_of[m][:, i, :],
+                    func=ACT.Identity,
+                    scale=rstd_of[m][:, i : i + 1],
+                    bias=shift_of[m][:, i - GPSIMD_TILES : i - GPSIMD_TILES + 1],
+                )
+
         def transpose(m):
-            planes_ps_of[m] = [
-                psum_t.tile([P, MACRO], F32, tag="plane", name="plane_ps%d" % j) for j in range(PACK)
-            ]
+            planes_ps_of[m] = [bank("plane_ps%d" % j) for j in range(PACK)]
             for j in range(PACK):
                 for i in range(TILES):
                     nc.tensor.transpose(
@@ -230,9 +255,9 @@ def tile_transformerlayershard_pa_t_kernel(
 
         def project(m, pair):
             first = 2 * pair
-            v_ps = psum_o.tile([P, 512], F32, tag="out")
-            pass_ps = [psum_o.tile([P, 512], F32, tag="out", name="pass_ps%d" % n) for n in range(2)]
-            rope_ps = psum_o.tile([P, 512], F32, tag="out")
+            v_ps = bank("v_ps")
+            pass_ps = [bank("pass_ps%d" % n) for n in range(2)]
+            rope_ps = bank("rope_ps")
             banks_of[(m, pair)] = (v_ps, pass_ps, rope_ps)
             for n in range(2):
                 one_pass(m, first + n, v_ps[:, n * V_COLS : (n + 1) * V_COLS], V_AT, V_COLS)
@@ -245,7 +270,7 @@ def tile_transformerlayershard_pa_t_kernel(
         def copy_out(m, pair):
             first = 2 * pair
             if pair == 0:
-                stage_of[m] = stage_pool.tile([P, 3, TILES, E], F32, name="stage")
+                stage_of[m] = out_pool.tile([P, 3, TILES, E], F32, name="stage")
             stage = stage_of[m]
             v_ps, pass_ps, rope_ps = banks_of[(m, pair)]
             nc.scalar.copy(out=stage[:, 2, first : first + 2, :].rearrange("p i c -> p (i c)"), in_=v_ps[:])
@@ -258,7 +283,7 @@ def tile_transformerlayershard_pa_t_kernel(
         def rope_products(m, pair):
             first = 2 * pair
             if pair == 0:
-                products_of[m] = work.tile([P, TILES, 2, HEADS_QK, ROT], F32, name="products")
+                products_of[m] = out_pool.tile([P, TILES, 2, HEADS_QK, ROT], F32, name="products")
             v_ps, pass_ps, rope_ps = banks_of[(m, pair)]
             pos = (m % POS_MACRO) * TILES + first
             nc.vector.tensor_tensor(
@@ -271,6 +296,9 @@ def tile_transformerlayershard_pa_t_kernel(
                 op=ALU.mult,
             )
 
+        def store(m, o):
+            nc.sync.dma_start(out=out_rows[o][m], in_=stage_of[m][:, o, :, :].rearrange("p i c -> p (i c)"))
+
         def rotate_and_store(m):
             for o in range(2):
                 nc.gpsimd.tensor_tensor(
@@ -279,8 +307,7 @@ def tile_transformerlayershard_pa_t_kernel(
                     in1=products_of[m][:, :, 1, o * H : (o + 1) * H, :],
                     op=ALU.add,
                 )
-            for o in range(3):
-                nc.sync.dma_start(out=out_rows[o][m], in_=stage_of[m][:, o, :, :].rearrange("p i c -> p (i c)"))
+                store(m, o)
 
         def when(m, stage, *args):
             if 0 <= m < N_MACRO:
@@ -289,23 +316,29 @@ def tile_transformerlayershard_pa_t_kernel(
         for s in range(-LOAD_AHEAD, N_MACRO + 1):
             if s + LOAD_AHEAD > 0:
                 when(s + LOAD_AHEAD, load)
-            when(s, project, 0)
-            when(s, copy_out, 0)
-            when(s + RSTD_AHEAD, std_dev)
-            if s + RSTD_AHEAD == 0:
-                regroup_weights()
-            when(s + PLANES_AHEAD, transpose)
-            when(s - 1, rotate_and_store)
-            when(s + Z_AHEAD, normalise)
-            when(s + QUANT_AHEAD, regroup)
             when(s, rope_products, 0)
-            when(s + RSTD_AHEAD, inverse_std)
-            when(s + PLANES_AHEAD, scale_shift)
+            when(s, copy_out, 0)
             when(s, project, 1)
+            when(s + NORM_AHEAD, std_dev)
+            when(s + NORM_AHEAD, negate_mean)
+            if 0 <= s + STATS_AHEAD < 3:
+                regroup_weights(s + STATS_AHEAD)
+            when(s + QUANT_AHEAD, regroup)
             when(s + STATS_AHEAD, token_stats, 0)
+            when(s + NORM_AHEAD, inverse_std)
+            when(s + NORM_AHEAD, normalise_on_gpsimd)
+            when(s + PLANES_AHEAD, scale_shift)
             when(s + QUANT_AHEAD, quantise)
+            when(s + QUANT_AHEAD, project, 0)
+            when(s + STATS_AHEAD, token_stats, 1)
+            when(s + NORM_AHEAD, normalise_on_scalar)
             when(s, rope_products, 1)
             when(s, copy_out, 1)
-            when(s + STATS_AHEAD, token_stats, 1)
+            when(s, store, 2)
+            when(s - 1, rotate_and_store)
+            when(s + STATS_AHEAD, token_stats, 2)
+            when(s + NORM_AHEAD, transpose)
+            when(s + STATS_AHEAD, token_stats, 3)
+            when(s + STATS_AHEAD, mean_and_variance)
             if s + PLANES_AHEAD == 0:
                 quantise_weights()

@@ -42,8 +42,6 @@ NORM_AHEAD = 3
 PLANES_AHEAD = 2
 QUANT_AHEAD = 1
 
-GPSIMD_TILES = 3
-
 
 def tile_transformerlayershard_pa_t_kernel(
     tc, x, ln_scale, ln_offset, wq, wk, wv, rope_cos, rope_sin, out_0, out_1, out_2
@@ -68,7 +66,7 @@ def tile_transformerlayershard_pa_t_kernel(
         def bank(name):
             return psum.tile([P, BANK], F32, tag="bank", name=name)
 
-        x_of, stats_of, mean_var_of, var_eps_of, std_of, rstd_of, neg_mean_of, shift_of = {}, {}, {}, {}, {}, {}, {}, {}
+        x_of, stats_of, mean_var_of, var_eps_of, std_of, rstd_of, neg_mean_of = {}, {}, {}, {}, {}, {}, {}
         z_of, planes_ps_of, planes_of, grouped_of, codes_of, scales_of = {}, {}, {}, {}, {}, {}
         banks_of, stage_of, products_of = {}, {}, {}
 
@@ -180,14 +178,7 @@ def tile_transformerlayershard_pa_t_kernel(
 
         def normalise_on_gpsimd(m):
             z_of[m] = z_pool.tile([P, TILES, D], F32, name="z")
-            shift_of[m] = small.tile([P, TILES - GPSIMD_TILES], F32, name="shift")
-            nc.gpsimd.tensor_tensor(
-                out=shift_of[m][:],
-                in0=neg_mean_of[m][:, GPSIMD_TILES:TILES],
-                in1=rstd_of[m][:, GPSIMD_TILES:TILES],
-                op=ALU.mult,
-            )
-            for i in range(GPSIMD_TILES):
+            for i in range(TILES):
                 nc.gpsimd.tensor_scalar(
                     out=z_of[m][:, i, :],
                     in0=x_of[m][:, i, :],
@@ -195,16 +186,6 @@ def tile_transformerlayershard_pa_t_kernel(
                     scalar2=rstd_of[m][:, i : i + 1],
                     op0=ALU.add,
                     op1=ALU.mult,
-                )
-
-        def normalise_on_scalar(m):
-            for i in range(GPSIMD_TILES, TILES):
-                nc.scalar.activation(
-                    out=z_of[m][:, i, :],
-                    in_=x_of[m][:, i, :],
-                    func=ACT.Identity,
-                    scale=rstd_of[m][:, i : i + 1],
-                    bias=shift_of[m][:, i - GPSIMD_TILES : i - GPSIMD_TILES + 1],
                 )
 
         def transpose(m):
@@ -331,7 +312,6 @@ def tile_transformerlayershard_pa_t_kernel(
             when(s + QUANT_AHEAD, quantise)
             when(s + QUANT_AHEAD, project, 0)
             when(s + STATS_AHEAD, token_stats, 1)
-            when(s + NORM_AHEAD, normalise_on_scalar)
             when(s, rope_products, 1)
             when(s, copy_out, 1)
             when(s, store, 2)

@@ -42,6 +42,8 @@ NORM_AHEAD = 3
 PLANES_AHEAD = 2
 QUANT_AHEAD = 1
 
+GPSIMD_TILES = 3
+
 
 def tile_transformerlayershard_pa_t_kernel(
     tc, x, ln_scale, ln_offset, wq, wk, wv, rope_cos, rope_sin, out_0, out_1, out_2
@@ -66,7 +68,7 @@ def tile_transformerlayershard_pa_t_kernel(
         def bank(name):
             return psum.tile([P, BANK], F32, tag="bank", name=name)
 
-        x_of, stats_of, mean_var_of, var_eps_of, std_of, rstd_of, neg_mean_of = {}, {}, {}, {}, {}, {}, {}
+        x_of, stats_of, mean_var_of, var_eps_of, std_of, rstd_of, neg_mean_of, shift_of = {}, {}, {}, {}, {}, {}, {}, {}
         z_of, planes_ps_of, planes_of, grouped_of, codes_of, scales_of = {}, {}, {}, {}, {}, {}
         banks_of, stage_of, products_of = {}, {}, {}
 
@@ -76,6 +78,22 @@ def tile_transformerlayershard_pa_t_kernel(
 
         load(0)
 
+        affine_rows = const.tile([P, P], BF16)
+        nc.vector.memset(affine_rows[:], 0.0)
+        nc.scalar.dma_start(out=affine_rows[0:PACK, :], in_=ln_scale.rearrange("(j p) -> j p", p=P))
+        nc.scalar.dma_start(out=affine_rows[PACK : 2 * PACK, :], in_=ln_offset.rearrange("(j p) -> j p", p=P))
+        rot_raw = []
+        for c, table in enumerate((rope_cos, rope_sin)):
+            raw = const.tile([P, POS_MACRO, TILES * HALF], BF16, name="rot_raw%d" % c)
+            nc.scalar.dma_start(out=raw[:], in_=table.rearrange("(m p i) a -> p m (i a)", p=P, i=TILES))
+            rot_raw.append(raw)
+
+        w_raw = []
+        for o, w in enumerate((wq, wk, wv)):
+            w_sb = const.tile([P, PACK, E], BF16, name="w_raw%d" % o)
+            nc.sync.dma_start(out=w_sb[:], in_=w.rearrange("(j p) n -> p j n", p=P))
+            w_raw.append(w_sb)
+
         one_col = const.tile([P, 1], F32)
         nc.vector.memset(one_col[:], 1.0)
         first_sqrt = const.tile([P, 1], F32)
@@ -84,16 +102,6 @@ def tile_transformerlayershard_pa_t_kernel(
         ident = const.tile([P, P], F32)
         make_identity(nc, ident[:])
 
-        w_raw = []
-        for o, w in enumerate((wq, wk, wv)):
-            w_sb = const.tile([P, PACK, E], BF16, name="w_raw%d" % o)
-            nc.sync.dma_start(out=w_sb[:], in_=w.rearrange("(j p) n -> p j n", p=P))
-            w_raw.append(w_sb)
-
-        affine_rows = const.tile([P, P], BF16)
-        nc.vector.memset(affine_rows[:], 0.0)
-        nc.scalar.dma_start(out=affine_rows[0:PACK, :], in_=ln_scale.rearrange("(j p) -> j p", p=P))
-        nc.scalar.dma_start(out=affine_rows[PACK : 2 * PACK, :], in_=ln_offset.rearrange("(j p) -> j p", p=P))
         affine_rows_f32 = const.tile([P, P], F32)
         nc.scalar.copy(out=affine_rows_f32[:], in_=affine_rows[:])
         affine_ps = bank("affine_ps")
@@ -102,12 +110,10 @@ def tile_transformerlayershard_pa_t_kernel(
         nc.scalar.copy(out=affine[:], in_=affine_ps[:, 0 : 2 * PACK])
 
         rot = const.tile([P, POS_MACRO * TILES, 2, ROT], F32)
-        for c, table in enumerate((rope_cos, rope_sin)):
-            raw = const.tile([P, POS_MACRO, TILES * HALF], BF16, name="rot_raw%d" % c)
-            nc.scalar.dma_start(out=raw[:], in_=table.rearrange("(m p i) a -> p m (i a)", p=P, i=TILES))
+        for c in range(2):
             nc.scalar.copy(
                 out=rot[:, :, c, :].rearrange("p t (a e) -> p t a e", e=2),
-                in_=raw[:]
+                in_=rot_raw[c][:]
                 .rearrange("p m (i a) -> p (m i) a", a=HALF)
                 .unsqueeze(3)
                 .to_broadcast([P, POS_MACRO * TILES, HALF, 2]),
@@ -178,7 +184,14 @@ def tile_transformerlayershard_pa_t_kernel(
 
         def normalise_on_gpsimd(m):
             z_of[m] = z_pool.tile([P, TILES, D], F32, name="z")
-            for i in range(TILES):
+            shift_of[m] = small.tile([P, TILES - GPSIMD_TILES], F32, name="shift")
+            nc.gpsimd.tensor_tensor(
+                out=shift_of[m][:],
+                in0=neg_mean_of[m][:, GPSIMD_TILES:TILES],
+                in1=rstd_of[m][:, GPSIMD_TILES:TILES],
+                op=ALU.mult,
+            )
+            for i in range(GPSIMD_TILES):
                 nc.gpsimd.tensor_scalar(
                     out=z_of[m][:, i, :],
                     in0=x_of[m][:, i, :],
@@ -186,6 +199,16 @@ def tile_transformerlayershard_pa_t_kernel(
                     scalar2=rstd_of[m][:, i : i + 1],
                     op0=ALU.add,
                     op1=ALU.mult,
+                )
+
+        def normalise_on_scalar(m):
+            for i in range(GPSIMD_TILES, TILES):
+                nc.scalar.activation(
+                    out=z_of[m][:, i, :],
+                    in_=x_of[m][:, i, :],
+                    func=ACT.Identity,
+                    scale=rstd_of[m][:, i : i + 1],
+                    bias=shift_of[m][:, i - GPSIMD_TILES : i - GPSIMD_TILES + 1],
                 )
 
         def transpose(m):
@@ -236,17 +259,17 @@ def tile_transformerlayershard_pa_t_kernel(
 
         def project(m, pair):
             first = 2 * pair
+            rope_ps = bank("rope_ps")
             v_ps = bank("v_ps")
             pass_ps = [bank("pass_ps%d" % n) for n in range(2)]
-            rope_ps = bank("rope_ps")
             banks_of[(m, pair)] = (v_ps, pass_ps, rope_ps)
+            for n in range(2):
+                one_pass(m, first + n, rope_ps[:, n * ROPE_COLS : (n + 1) * ROPE_COLS], ROPE_AT, ROPE_COLS)
             for n in range(2):
                 one_pass(m, first + n, v_ps[:, n * V_COLS : (n + 1) * V_COLS], V_AT, V_COLS)
             for n in range(2):
                 one_pass(m, first + n, pass_ps[n][:, 0:256], PASS_AT, 256)
                 one_pass(m, first + n, pass_ps[n][:, 256:PASS_COLS], PASS_AT + 256, PASS_COLS - 256)
-            for n in range(2):
-                one_pass(m, first + n, rope_ps[:, n * ROPE_COLS : (n + 1) * ROPE_COLS], ROPE_AT, ROPE_COLS)
 
         def copy_out(m, pair):
             first = 2 * pair
@@ -297,26 +320,27 @@ def tile_transformerlayershard_pa_t_kernel(
         for s in range(-LOAD_AHEAD, N_MACRO + 1):
             if s + LOAD_AHEAD > 0:
                 when(s + LOAD_AHEAD, load)
-            when(s, rope_products, 0)
-            when(s, copy_out, 0)
-            when(s, project, 1)
             when(s + NORM_AHEAD, std_dev)
             when(s + NORM_AHEAD, negate_mean)
             if 0 <= s + STATS_AHEAD < 3:
                 regroup_weights(s + STATS_AHEAD)
+            when(s - 1, rotate_and_store)
             when(s + QUANT_AHEAD, regroup)
-            when(s + STATS_AHEAD, token_stats, 0)
+            when(s, rope_products, 0)
+            when(s, copy_out, 0)
+            when(s, project, 1)
+            when(s + QUANT_AHEAD, quantise)
             when(s + NORM_AHEAD, inverse_std)
             when(s + NORM_AHEAD, normalise_on_gpsimd)
-            when(s + PLANES_AHEAD, scale_shift)
-            when(s + QUANT_AHEAD, quantise)
-            when(s + QUANT_AHEAD, project, 0)
+            when(s + STATS_AHEAD, token_stats, 0)
             when(s + STATS_AHEAD, token_stats, 1)
+            when(s + PLANES_AHEAD, scale_shift)
+            when(s + QUANT_AHEAD, project, 0)
+            when(s + STATS_AHEAD, token_stats, 2)
+            when(s + NORM_AHEAD, normalise_on_scalar)
             when(s, rope_products, 1)
             when(s, copy_out, 1)
             when(s, store, 2)
-            when(s - 1, rotate_and_store)
-            when(s + STATS_AHEAD, token_stats, 2)
             when(s + NORM_AHEAD, transpose)
             when(s + STATS_AHEAD, token_stats, 3)
             when(s + STATS_AHEAD, mean_and_variance)

@@ -68,7 +68,7 @@ def tile_transformerlayershard_pa_t_kernel(
         def bank(name):
             return psum.tile([P, BANK], F32, tag="bank", name=name)
 
-        x_of, stats_of, mean_var_of, var_eps_of, std_of, rstd_of, neg_mean_of, shift_of = {}, {}, {}, {}, {}, {}, {}, {}
+        x_of, stats_of, mean_var_of, std_of, rstd_of, neg_mean_of, shift_of = {}, {}, {}, {}, {}, {}, {}
         z_of, planes_ps_of, planes_of, grouped_of, codes_of, scales_of = {}, {}, {}, {}, {}, {}
         banks_of, stage_of, products_of = {}, {}, {}
 
@@ -98,6 +98,8 @@ def tile_transformerlayershard_pa_t_kernel(
         nc.vector.memset(one_col[:], 1.0)
         first_sqrt = const.tile([P, 1], F32)
         nc.scalar.activation(out=first_sqrt[:], in_=one_col[:], func=ACT.Sqrt)
+        eps_col = const.tile([P, 1], F32)
+        nc.vector.tensor_scalar(out=eps_col[:], in0=one_col[:], scalar1=EPS, scalar2=None, op0=ALU.mult)
 
         ident = const.tile([P, P], F32)
         make_identity(nc, ident[:])
@@ -111,12 +113,16 @@ def tile_transformerlayershard_pa_t_kernel(
 
         rot = const.tile([P, POS_MACRO * TILES, 2, ROT], F32)
         for c in range(2):
-            nc.scalar.copy(
+            nc.gpsimd.tensor_scalar(
                 out=rot[:, :, c, :].rearrange("p t (a e) -> p t a e", e=2),
-                in_=rot_raw[c][:]
+                in0=rot_raw[c][:]
                 .rearrange("p m (i a) -> p (m i) a", a=HALF)
                 .unsqueeze(3)
                 .to_broadcast([P, POS_MACRO * TILES, HALF, 2]),
+                scalar1=1.0,
+                scalar2=0.0,
+                op0=ALU.mult,
+                op1=ALU.add,
             )
 
         w_grouped = const.tile([P, W_COLS, PACK], BF16, align_bytes=64)
@@ -125,23 +131,27 @@ def tile_transformerlayershard_pa_t_kernel(
 
         def regroup_weights(o):
             if o == 2:
-                nc.scalar.copy(out=w_grouped[:, V_AT : V_AT + V_COLS, :], in_=w_raw[2][:].rearrange("p j n -> p n j"))
+                nc.vector.tensor_copy(
+                    out=w_grouped[:, V_AT : V_AT + V_COLS, :], in_=w_raw[2][:].rearrange("p j n -> p n j")
+                )
                 return
             by_col = w_raw[o][:].rearrange("p j (h d) -> p h d j", h=H)
             head_cols = H * ROT
             plain_at = ROPE_AT + o * head_cols
-            nc.scalar.copy(
+            nc.vector.tensor_copy(
                 out=w_grouped[:, plain_at : plain_at + head_cols, :].rearrange("p (h f) j -> p h f j", h=H),
                 in_=by_col[:, :, 0:ROT, :],
             )
             swap_at = ROPE_AT + HEADS_QK * ROT + o * head_cols
             swapped = w_grouped[:, swap_at : swap_at + head_cols, :].rearrange("p (h a e) j -> p h a e j", h=H, e=2)
             pairs = by_col[:, :, 0:ROT, :].rearrange("p h (a e) j -> p h a e j", e=2)
-            nc.scalar.mul(out=swapped[:, :, :, 0, :], in_=pairs[:, :, :, 1, :], mul=-1.0)
-            nc.scalar.copy(out=swapped[:, :, :, 1, :], in_=pairs[:, :, :, 0, :])
+            nc.vector.tensor_scalar(
+                out=swapped[:, :, :, 0, :], in0=pairs[:, :, :, 1, :], scalar1=-1.0, scalar2=None, op0=ALU.mult
+            )
+            nc.vector.tensor_copy(out=swapped[:, :, :, 1, :], in_=pairs[:, :, :, 0, :])
             pass_cols = H * (DH - ROT)
             pass_at = PASS_AT + o * pass_cols
-            nc.scalar.copy(
+            nc.vector.tensor_copy(
                 out=w_grouped[:, pass_at : pass_at + pass_cols, :].rearrange("p (h d) j -> p h d j", h=H),
                 in_=by_col[:, :, ROT:DH, :],
             )
@@ -163,14 +173,10 @@ def tile_transformerlayershard_pa_t_kernel(
             mean_var_of[m] = small.tile([P, TILES, 2], F32, name="mean_var")
             for i in range(TILES):
                 nc.vector.bn_aggr(out=mean_var_of[m][:, i, :], in_=stats_of[m][:, i, :])
-            var_eps_of[m] = small.tile([P, TILES], F32, name="var_eps")
-            nc.vector.tensor_scalar(
-                out=var_eps_of[m][:], in0=mean_var_of[m][:, :, 1], scalar1=EPS, scalar2=None, op0=ALU.add
-            )
 
         def std_dev(m):
             std_of[m] = small.tile([P, TILES], F32, name="std")
-            nc.scalar.activation(out=std_of[m][:], in_=var_eps_of[m][:], func=ACT.Sqrt)
+            nc.scalar.activation(out=std_of[m][:], in_=mean_var_of[m][:, :, 1], func=ACT.Sqrt, bias=eps_col[:])
 
         def negate_mean(m):
             neg_mean_of[m] = small.tile([P, TILES], F32, name="neg_mean")
@@ -322,8 +328,6 @@ def tile_transformerlayershard_pa_t_kernel(
                 when(s + LOAD_AHEAD, load)
             when(s + NORM_AHEAD, std_dev)
             when(s + NORM_AHEAD, negate_mean)
-            if 0 <= s + STATS_AHEAD < 3:
-                regroup_weights(s + STATS_AHEAD)
             when(s - 1, rotate_and_store)
             when(s + QUANT_AHEAD, regroup)
             when(s, rope_products, 0)
@@ -344,5 +348,7 @@ def tile_transformerlayershard_pa_t_kernel(
             when(s + NORM_AHEAD, transpose)
             when(s + STATS_AHEAD, token_stats, 3)
             when(s + STATS_AHEAD, mean_and_variance)
+            if 0 <= s + STATS_AHEAD < 3:
+                regroup_weights(s + STATS_AHEAD)
             if s + PLANES_AHEAD == 0:
                 quantise_weights()

@@ -227,13 +227,24 @@ def tile_transformerlayershard_pa_t_kernel(
 
         def scale_shift(m):
             planes_of[m] = work.tile([P, PACK, MACRO], BF16, name="xn_planes")
-            for j in range(PACK):
+            vector_is_free = m - PLANES_AHEAD + STATS_AHEAD >= N_MACRO
+            scalar_planes = PACK // 2 if vector_is_free else PACK
+            for j in range(scalar_planes):
                 nc.scalar.activation(
                     out=planes_of[m][:, j, :],
                     in_=planes_ps_of[m][j][:],
                     func=ACT.Identity,
                     scale=affine[:, j : j + 1],
                     bias=affine[:, PACK + j : PACK + j + 1],
+                )
+            for j in range(scalar_planes, PACK):
+                nc.vector.tensor_scalar(
+                    out=planes_of[m][:, j, :],
+                    in0=planes_ps_of[m][j][:],
+                    scalar1=affine[:, j : j + 1],
+                    scalar2=affine[:, PACK + j : PACK + j + 1],
+                    op0=ALU.mult,
+                    op1=ALU.add,
                 )
 
         def regroup(m):

from contextlib import ExitStack

import concourse.mybir as mybir
from concourse.masks import make_identity

F32 = mybir.dt.float32
BF16 = mybir.dt.bfloat16
U32 = mybir.dt.uint32
U8 = mybir.dt.uint8
FP8X4 = mybir.dt.float8_e4m3fn_x4
ALU = mybir.AluOpType
ACT = mybir.ActivationFunctionType

P = 128
PACK = 4
BANK = 512
BANKS = 8
B, T, D, H, DH, ROT = 2, 4096, 512, 2, 128, 32
E = H * DH
EPS = 1e-5
TOKENS = B * T
TILES = 4
MACRO = P * TILES
N_MACRO = TOKENS // MACRO
POS_MACRO = T // MACRO
HALF = ROT // 2
HEADS_QK = 2 * H

ROPE_COLS = 2 * HEADS_QK * ROT
V_COLS = E
PASS_COLS = HEADS_QK * (DH - ROT)
ROPE_AT = 0
V_AT = ROPE_AT + ROPE_COLS
PASS_AT = V_AT + V_COLS
W_COLS = PASS_AT + PASS_COLS

FLOPS = 2 * TOKENS * D * 3 * E

LOAD_AHEAD = 6
STATS_AHEAD = 4
NORM_AHEAD = 3
PLANES_AHEAD = 2
QUANT_AHEAD = 1

GPSIMD_TILES = 3


def tile_transformerlayershard_pa_t_kernel(
    tc, x, ln_scale, ln_offset, wq, wk, wv, rope_cos, rope_sin, out_0, out_1, out_2
):
    nc = tc.nc
    x_rows = x.rearrange("b t k -> (b t) k").rearrange("(m p i) k -> m p (i k)", p=P, i=TILES)
    out_rows = [
        o.rearrange("b t h d -> (b t) (h d)").rearrange("(m p i) c -> m p (i c)", p=P, i=TILES)
        for o in (out_0, out_1, out_2)
    ]

    with ExitStack() as ctx:
        const = ctx.enter_context(tc.tile_pool(name="const", bufs=1))
        x_pool = ctx.enter_context(tc.tile_pool(name="x", bufs=5))
        small = ctx.enter_context(tc.tile_pool(name="small", bufs=4))
        z_pool = ctx.enter_context(tc.tile_pool(name="z", bufs=3))
        work = ctx.enter_context(tc.tile_pool(name="work", bufs=2))
        out_pool = ctx.enter_context(tc.tile_pool(name="out", bufs=3))
        psum = ctx.enter_context(tc.psum_pool(name="psum", bufs=BANKS))
        ctx.enter_context(tc.manual_schedule())

        def bank(name):
            return psum.tile([P, BANK], F32, tag="bank", name=name)

        x_of, stats_of, mean_var_of, std_of, rstd_of, neg_mean_of, shift_of = {}, {}, {}, {}, {}, {}, {}
        z_of, planes_ps_of, planes_of, grouped_of, codes_of, scales_of = {}, {}, {}, {}, {}, {}
        banks_of, stage_of, products_of = {}, {}, {}

        def load(m):
            x_of[m] = x_pool.tile([P, TILES, D], BF16, name="x_sb")
            nc.sync.dma_start(out=x_of[m][:].rearrange("p i k -> p (i k)"), in_=x_rows[m])

        load(0)

        affine_rows = const.tile([P, P], BF16)
        nc.vector.memset(affine_rows[:], 0.0)
        nc.scalar.dma_start(out=affine_rows[0:PACK, :], in_=ln_scale.rearrange("(j p) -> j p", p=P))
        nc.scalar.dma_start(out=affine_rows[PACK : 2 * PACK, :], in_=ln_offset.rearrange("(j p) -> j p", p=P))
        rot_raw = []
        for c, table in enumerate((rope_cos, rope_sin)):
            raw = const.tile([P, POS_MACRO, TILES * HALF], BF16, name="rot_raw%d" % c)
            nc.scalar.dma_start(out=raw[:], in_=table.rearrange("(m p i) a -> p m (i a)", p=P, i=TILES))
            rot_raw.append(raw)

        w_raw = []
        for o, w in enumerate((wq, wk, wv)):
            w_sb = const.tile([P, PACK, E], BF16, name="w_raw%d" % o)
            nc.sync.dma_start(out=w_sb[:], in_=w.rearrange("(j p) n -> p j n", p=P))
            w_raw.append(w_sb)

        one_col = const.tile([P, 1], F32)
        nc.vector.memset(one_col[:], 1.0)
        first_sqrt = const.tile([P, 1], F32)
        nc.scalar.activation(out=first_sqrt[:], in_=one_col[:], func=ACT.Sqrt)
        eps_col = const.tile([P, 1], F32)
        nc.vector.tensor_scalar(out=eps_col[:], in0=one_col[:], scalar1=EPS, scalar2=None, op0=ALU.mult)

        ident = const.tile([P, P], F32)
        make_identity(nc, ident[:])

        affine_rows_f32 = const.tile([P, P], F32)
        nc.scalar.copy(out=affine_rows_f32[:], in_=affine_rows[:])
        affine_ps = bank("affine_ps")
        nc.tensor.transpose(affine_ps[:, 0:P], affine_rows_f32[:], ident[:])
        affine = const.tile([P, 2 * PACK], F32)
        nc.scalar.copy(out=affine[:], in_=affine_ps[:, 0 : 2 * PACK])

        rot = const.tile([P, POS_MACRO * TILES, 2, ROT], F32)
        for c in range(2):
            nc.gpsimd.tensor_scalar(
                out=rot[:, :, c, :].rearrange("p t (a e) -> p t a e", e=2),
                in0=rot_raw[c][:]
                .rearrange("p m (i a) -> p (m i) a", a=HALF)
                .unsqueeze(3)
                .to_broadcast([P, POS_MACRO * TILES, HALF, 2]),
                scalar1=1.0,
                scalar2=0.0,
                op0=ALU.mult,
                op1=ALU.add,
            )

        w_grouped = const.tile([P, W_COLS, PACK], BF16, align_bytes=64)
        w_codes = const.tile([P, W_COLS], U32, align_bytes=64)
        w_scales = const.tile([P, W_COLS], U8, align_bytes=64)

        def regroup_weights(o):
            if o == 2:
                nc.vector.tensor_copy(
                    out=w_grouped[:, V_AT : V_AT + V_COLS, :], in_=w_raw[2][:].rearrange("p j n -> p n j")
                )
                return
            by_col = w_raw[o][:].rearrange("p j (h d) -> p h d j", h=H)
            head_cols = H * ROT
            plain_at = ROPE_AT + o * head_cols
            nc.vector.tensor_copy(
                out=w_grouped[:, plain_at : plain_at + head_cols, :].rearrange("p (h f) j -> p h f j", h=H),
                in_=by_col[:, :, 0:ROT, :],
            )
            swap_at = ROPE_AT + HEADS_QK * ROT + o * head_cols
            swapped = w_grouped[:, swap_at : swap_at + head_cols, :].rearrange("p (h a e) j -> p h a e j", h=H, e=2)
            pairs = by_col[:, :, 0:ROT, :].rearrange("p h (a e) j -> p h a e j", e=2)
            nc.vector.tensor_scalar(
                out=swapped[:, :, :, 0, :], in0=pairs[:, :, :, 1, :], scalar1=-1.0, scalar2=None, op0=ALU.mult
            )
            nc.vector.tensor_copy(out=swapped[:, :, :, 1, :], in_=pairs[:, :, :, 0, :])
            pass_cols = H * (DH - ROT)
            pass_at = PASS_AT + o * pass_cols
            nc.vector.tensor_copy(
                out=w_grouped[:, pass_at : pass_at + pass_cols, :].rearrange("p (h d) j -> p h d j", h=H),
                in_=by_col[:, :, ROT:DH, :],
            )

        def quantise_weights():
            for lo, hi in ((0, 512), (512, 768), (768, 896)):
                nc.vector.quantize_mx(
                    out=w_codes[:, lo:hi].bitcast(FP8X4),
                    scales=w_scales[:, lo:hi],
                    in_=w_grouped[:, lo:hi, :].rearrange("p c j -> p (c j)"),
                )

        def token_stats(m, i):
            if i == 0:
                stats_of[m] = small.tile([P, TILES, 6], F32, name="stats")
            nc.vector.bn_stats(out=stats_of[m][:, i, :], in_=x_of[m][:, i, :])

        def mean_and_variance(m):
            mean_var_of[m] = small.tile([P, TILES, 2], F32, name="mean_var")
            for i in range(TILES):
                nc.vector.bn_aggr(out=mean_var_of[m][:, i, :], in_=stats_of[m][:, i, :])

        def std_dev(m):
            std_of[m] = small.tile([P, TILES], F32, name="std")
            nc.scalar.activation(out=std_of[m][:], in_=mean_var_of[m][:, :, 1], func=ACT.Sqrt, bias=eps_col[:])

        def negate_mean(m):
            neg_mean_of[m] = small.tile([P, TILES], F32, name="neg_mean")
            nc.gpsimd.tensor_scalar(
                out=neg_mean_of[m][:], in0=mean_var_of[m][:, :, 0], scalar1=-1.0, scalar2=0.0, op0=ALU.mult, op1=ALU.add
            )

        def inverse_std(m):
            rstd_of[m] = small.tile([P, TILES], F32, name="rstd")
            nc.vector.reciprocal(out=rstd_of[m][:], in_=std_of[m][:])

        def normalise_on_gpsimd(m):
            z_of[m] = z_pool.tile([P, TILES, D], F32, name="z")
            shift_of[m] = small.tile([P, TILES - GPSIMD_TILES], F32, name="shift")
            nc.gpsimd.tensor_tensor(
                out=shift_of[m][:],
                in0=neg_mean_of[m][:, GPSIMD_TILES:TILES],
                in1=rstd_of[m][:, GPSIMD_TILES:TILES],
                op=ALU.mult,
            )
            for i in range(GPSIMD_TILES):
                nc.gpsimd.tensor_scalar(
                    out=z_of[m][:, i, :],
                    in0=x_of[m][:, i, :],
                    scalar1=neg_mean_of[m][:, i : i + 1],
                    scalar2=rstd_of[m][:, i : i + 1],
                    op0=ALU.add,
                    op1=ALU.mult,
                )

        def normalise_on_scalar(m):
            for i in range(GPSIMD_TILES, TILES):
                nc.scalar.activation(
                    out=z_of[m][:, i, :],
                    in_=x_of[m][:, i, :],
                    func=ACT.Identity,
                    scale=rstd_of[m][:, i : i + 1],
                    bias=shift_of[m][:, i - GPSIMD_TILES : i - GPSIMD_TILES + 1],
                )

        def transpose(m):
            planes_ps_of[m] = [bank("plane_ps%d" % j) for j in range(PACK)]
            for j in range(PACK):
                for i in range(TILES):
                    nc.tensor.transpose(
                        planes_ps_of[m][j][:, i * P : (i + 1) * P], z_of[m][:, i, j * P : (j + 1) * P], ident[:]
                    )

        def scale_shift(m):
            planes_of[m] = work.tile([P, PACK, MACRO], BF16, name="xn_planes")
            vector_is_free = m - PLANES_AHEAD + STATS_AHEAD >= N_MACRO
            scalar_planes = PACK // 2 if vector_is_free else PACK
            for j in range(scalar_planes):
                nc.scalar.activation(
                    out=planes_of[m][:, j, :],
                    in_=planes_ps_of[m][j][:],
                    func=ACT.Identity,
                    scale=affine[:, j : j + 1],
                    bias=affine[:, PACK + j : PACK + j + 1],
                )
            for j in range(scalar_planes, PACK):
                nc.vector.tensor_scalar(
                    out=planes_of[m][:, j, :],
                    in0=planes_ps_of[m][j][:],
                    scalar1=affine[:, j : j + 1],
                    scalar2=affine[:, PACK + j : PACK + j + 1],
                    op0=ALU.mult,
                    op1=ALU.add,
                )

        def regroup(m):
            grouped_of[m] = work.tile([P, MACRO, PACK], BF16, align_bytes=64, name="xn_grouped")
            nc.vector.tensor_copy(
                out=grouped_of[m][:].rearrange("p (c r) j -> p c j r", r=4),
                in_=planes_of[m][:].rearrange("p j (c r) -> p c j r", r=4),
            )

        def quantise(m):
            codes_of[m] = work.tile([P, MACRO], U32, align_bytes=64, name="xn_codes")
            scales_of[m] = work.tile([P, MACRO], U8, align_bytes=64, name="xn_scales")
            nc.vector.quantize_mx(
                out=codes_of[m][:].bitcast(FP8X4),
                scales=scales_of[m][:],
                in_=grouped_of[m][:].rearrange("p t j -> p (t j)"),
            )

        def one_pass(m, i, out_ps, at, cols):
            nc.tensor.matmul_mx(
                out=out_ps,
                lhsT=codes_of[m][:, i * P : (i + 1) * P].bitcast(FP8X4),
                lhsT_scale=scales_of[m][:, i * P : (i + 1) * P],
                rhs=w_codes[:, at : at + cols].bitcast(FP8X4),
                rhs_scale=w_scales[:, at : at + cols],
                start=True,
                stop=True,
            )

        def project(m, pair):
            first = 2 * pair
            rope_ps = bank("rope_ps")
            v_ps = bank("v_ps")
            pass_ps = [bank("pass_ps%d" % n) for n in range(2)]
            banks_of[(m, pair)] = (v_ps, pass_ps, rope_ps)
            for n in range(2):
                one_pass(m, first + n, rope_ps[:, n * ROPE_COLS : (n + 1) * ROPE_COLS], ROPE_AT, ROPE_COLS)
            for n in range(2):
                one_pass(m, first + n, v_ps[:, n * V_COLS : (n + 1) * V_COLS], V_AT, V_COLS)
            for n in range(2):
                one_pass(m, first + n, pass_ps[n][:, 0:256], PASS_AT, 256)
                one_pass(m, first + n, pass_ps[n][:, 256:PASS_COLS], PASS_AT + 256, PASS_COLS - 256)

        def copy_out(m, pair):
            first = 2 * pair
            if pair == 0:
                stage_of[m] = out_pool.tile([P, 3, TILES, E], F32, name="stage")
            stage = stage_of[m]
            v_ps, pass_ps, rope_ps = banks_of[(m, pair)]
            nc.scalar.copy(out=stage[:, 2, first : first + 2, :].rearrange("p i c -> p (i c)"), in_=v_ps[:])
            for n in range(2):
                nc.scalar.copy(
                    out=stage[:, 0:2, first + n, :].rearrange("p o (h d) -> p o h d", h=H)[:, :, :, ROT:DH],
                    in_=pass_ps[n][:, 0:PASS_COLS].rearrange("p (o h d) -> p o h d", o=2, h=H),
                )

        def rope_products(m, pair):
            first = 2 * pair
            if pair == 0:
                products_of[m] = out_pool.tile([P, TILES, 2, HEADS_QK, ROT], F32, name="products")
            v_ps, pass_ps, rope_ps = banks_of[(m, pair)]
            pos = (m % POS_MACRO) * TILES + first
            nc.vector.tensor_tensor(
                out=products_of[m][:, first : first + 2, :, :, :].rearrange("p i c g f -> p (i c) g f"),
                in0=rope_ps[:].rearrange("p (a g f) -> p a g f", g=HEADS_QK, f=ROT),
                in1=rot[:, pos : pos + 2, :, :]
                .rearrange("p i c f -> p (i c) f")
                .unsqueeze(2)
                .to_broadcast([P, 4, HEADS_QK, ROT]),
                op=ALU.mult,
            )

        def store(m, o):
            nc.sync.dma_start(out=out_rows[o][m], in_=stage_of[m][:, o, :, :].rearrange("p i c -> p (i c)"))

        def rotate_and_store(m):
            for o in range(2):
                nc.gpsimd.tensor_tensor(
                    out=stage_of[m][:, o, :, :].rearrange("p i (h d) -> p i h d", h=H)[:, :, :, 0:ROT],
                    in0=products_of[m][:, :, 0, o * H : (o + 1) * H, :],
                    in1=products_of[m][:, :, 1, o * H : (o + 1) * H, :],
                    op=ALU.add,
                )
                store(m, o)

        def when(m, stage, *args):
            if 0 <= m < N_MACRO:
                stage(m, *args)

        for s in range(-LOAD_AHEAD, N_MACRO + 1):
            if s + LOAD_AHEAD > 0:
                when(s + LOAD_AHEAD, load)
            when(s + NORM_AHEAD, std_dev)
            when(s + NORM_AHEAD, negate_mean)
            when(s - 1, rotate_and_store)
            when(s + QUANT_AHEAD, regroup)
            when(s, rope_products, 0)
            when(s, copy_out, 0)
            when(s, project, 1)
            when(s + QUANT_AHEAD, quantise)
            when(s + NORM_AHEAD, inverse_std)
            when(s + NORM_AHEAD, normalise_on_gpsimd)
            when(s + STATS_AHEAD, token_stats, 0)
            when(s + STATS_AHEAD, token_stats, 1)
            when(s + PLANES_AHEAD, scale_shift)
            when(s + QUANT_AHEAD, project, 0)
            when(s + STATS_AHEAD, token_stats, 2)
            when(s + NORM_AHEAD, normalise_on_scalar)
            when(s, rope_products, 1)
            when(s, copy_out, 1)
            when(s, store, 2)
            when(s + NORM_AHEAD, transpose)
            when(s + STATS_AHEAD, token_stats, 3)
            when(s + STATS_AHEAD, mean_and_variance)
            if 0 <= s + STATS_AHEAD < 3:
                regroup_weights(s + STATS_AHEAD)
            if s + PLANES_AHEAD == 0:
                quantise_weights()
